import numpy as np
import ml_dtypes


def mxq(x, axis, fmt="e4m3"):
    dtype, down = {"e4m3": (ml_dtypes.float8_e4m3fn, 7), "e5m2": (ml_dtypes.float8_e5m2, 14)}[fmt]
    v = np.moveaxis(np.asarray(x, np.float32).astype(ml_dtypes.bfloat16).astype(np.float64), axis, -1)
    blocks = v.reshape(v.shape[:-1] + (-1, 32))
    amax = np.abs(blocks).max(-1, keepdims=True)
    byte = np.maximum(np.where(amax > 0, np.frexp(amax)[1] - 1 + 127, 0) - down, 1)
    scale = np.exp2(byte - 127.0)
    codes = (blocks / scale).astype(np.float32).astype(dtype).astype(np.float64)
    return np.moveaxis((codes * scale).reshape(v.shape), -1, axis)


WIDE = False


def mx_kscale(k):
    if not WIDE:
        return np.ones(k)
    levels = np.array([10, -10, 5, -5, 0])
    if k % 512:
        return np.exp2(np.random.permutation(np.resize(levels, k // 32))).repeat(32)
    a = np.empty((k // 512, 16))
    for p in range(k // 512):
        a[p, :8] = np.random.permutation(np.resize(levels, 8))
        for g in range(8):
            far = levels[np.abs(levels - a[p, g]) >= 10]
            a[p, g + 8] = far[np.random.randint(len(far))]
    return np.exp2(a.ravel()).repeat(32)


BF16 = ml_dtypes.bfloat16


def bf(x):
    return np.asarray(x, np.float32).astype(BF16)


def f64(x):
    return np.asarray(x).astype(np.float64)


N, DIN, H1, H2, C, NC, G = 1024, 512, 512, 256, 128, 512, 8


def setup_inputs():
    s = mx_kscale(N)
    centres = np.random.standard_normal((G, C)) * 1.5
    z = centres[np.random.randint(G, size=N)] + 0.5 * np.random.standard_normal((N, C))
    return {"feats": bf(1.0 / (1.0 + np.exp(-z))),
            "pf_offdiag": bf(np.random.uniform(size=(N, N)) / np.sqrt(N) * (1.0 - np.eye(N)) * s),
            "members": bf((np.random.uniform(size=(N, NC)) < 0.1) * (0.5 + np.random.uniform(size=(N, NC))) / s[:, None])}


def reference(feats, pf_offdiag, members):
    sq = np.sum(f64(feats) * f64(feats), axis=-1)
    d2 = sq[:, None] + sq[None, :] - 2.0 * (f64(feats) @ f64(feats).T)
    dist = np.sqrt(np.maximum(d2, 1e-12))
    force = dist * f64(pf_offdiag)
    return mxq(force, 1, "e4m3") @ mxq(f64(members), 0, "e4m3")

@@ -1,0 +1,243 @@
+from contextlib import ExitStack
+
+import concourse.mybir as mybir
+from concourse.masks import make_identity
+
+F32 = mybir.dt.float32
+BF16 = mybir.dt.bfloat16
+U32 = mybir.dt.uint32
+U8 = mybir.dt.uint8
+FP8X4 = mybir.dt.float8_e4m3fn_x4
+ALU = mybir.AluOpType
+ACT = mybir.ActivationFunctionType
+
+NODES = 1024
+CODE = 128
+CLUSTERS = 512
+D2_FLOOR = 1e-12
+
+P = 128
+PACK = 4
+K_PASS = P * PACK
+PASSES = NODES // K_PASS
+TILES = NODES // P
+BANK = 512
+
+GROUP_TILES = 2
+GROUP = GROUP_TILES * P
+GROUPS = NODES // GROUP
+STEPS = GROUPS * PASSES
+BANK_TILES = BANK // GROUP
+PAIR = 2
+WORDS = PACK // PAIR
+
+LAG = 2
+
+FLOPS = 2 * NODES * NODES * CODE + 2 * NODES * NODES * CLUSTERS
+
+
+def tile_controencodnet_pb_kernel(tc, feats, pf_offdiag, members, out):
+    nc = tc.nc
+
+    feats_nodes = feats.rearrange("(g p w e) c -> p g w e c", g=PASSES, w=WORDS, e=PAIR)
+    pf_rows = pf_offdiag.rearrange("(g p w e) j -> p g w e j", g=PASSES, w=WORDS, e=PAIR)
+    members_nodes = members.rearrange("(g p w e) c -> p g w e c", g=PASSES, w=WORDS, e=PAIR)
+    out_rows = out.rearrange("(g p w e) c -> p g w e c", g=PASSES, w=WORDS, e=PAIR)
+
+    with ExitStack() as ctx:
+        ctx.enter_context(tc.manual_schedule())
+        keep = ctx.enter_context(tc.tile_pool(name="keep", bufs=1))
+        work = ctx.enter_context(tc.tile_pool(name="work", bufs=LAG + 1))
+        gram_psum = ctx.enter_context(tc.psum_pool(name="gram_psum", bufs=4))
+        pft_psum = ctx.enter_context(tc.psum_pool(name="pft_psum", bufs=2))
+        acc_psum = ctx.enter_context(tc.psum_pool(name="acc_psum", bufs=GROUP_TILES))
+
+        feats_sb = keep.tile([P, PASSES, PACK, CODE], BF16)
+        for g in range(PASSES):
+            nc.sync.dma_start(
+                out=feats_sb[:, g].rearrange("p (w e) c -> p w e c", e=PAIR), in_=feats_nodes[:, g]
+            )
+        members_sb = keep.tile([P, PASSES, PACK, CLUSTERS], BF16)
+        for g in range(PASSES):
+            nc.sync.dma_start(
+                out=members_sb[:, g].rearrange("p (w e) c -> p w e c", e=PAIR),
+                in_=members_nodes[:, g],
+            )
+        pf_sb = []
+        for q in range(GROUPS):
+            g_row, w_row = divmod(q, WORDS)
+            pf_group = keep.tile([P, GROUP_TILES, NODES], BF16, name="pf_group%d" % q)
+            nc.sync.dma_start(out=pf_group[:], in_=pf_rows[:, g_row, w_row])
+            pf_sb.append(pf_group)
+
+        one = keep.tile([P, 1], F32)
+        nc.vector.memset(one[:], 1.0)
+        nc.scalar.activation(out=one[:], in_=one[:], func=ACT.Sqrt)
+        ident_bf16 = keep.tile([P, P], BF16)
+        make_identity(nc, ident_bf16[:])
+        ident_f32 = keep.tile([P, P], F32)
+        make_identity(nc, ident_f32[:])
+
+        featsT = keep.tile([P, NODES], BF16)
+        featsT_m2 = keep.tile([P, NODES], BF16)
+        for g in range(PASSES):
+            featsT_ps = pft_psum.tile([P, K_PASS], BF16, tag="pft")
+            for t in range(PACK):
+                nc.tensor.transpose(
+                    featsT_ps[:, t * P : (t + 1) * P], feats_sb[:, g, t, :], ident_bf16[:]
+                )
+            pass_cols = slice(g * K_PASS, (g + 1) * K_PASS)
+            nc.vector.tensor_copy(out=featsT[:, pass_cols], in_=featsT_ps[:])
+            nc.vector.tensor_scalar_mul(out=featsT_m2[:, pass_cols], in0=featsT_ps[:], scalar1=-2.0)
+
+        squares = keep.tile([P, TILES, CODE], F32)
+        sq = keep.tile([P, TILES], F32)
+        for a in range(TILES):
+            g, t = divmod(a, PACK)
+            nc.scalar.activation(
+                out=squares[:, a, :],
+                in_=feats_sb[:, g, t, :],
+                func=ACT.Square,
+                accum_out=sq[:, a : a + 1],
+            )
+
+        members_grouped = keep.tile([P, PASSES, CLUSTERS, PACK], BF16, align_bytes=64)
+        for g in range(PASSES):
+            nc.gpsimd.tensor_scalar(
+                out=members_grouped[:, g],
+                in0=members_sb[:, g].rearrange("p t c -> p c t"),
+                scalar1=1.0,
+                scalar2=0.0,
+                op0=ALU.mult,
+                op1=ALU.add,
+            )
+        members_codes = keep.tile([P, PASSES, CLUSTERS], U32, align_bytes=64)
+        members_scales = keep.tile([P, PASSES, CLUSTERS], U8, align_bytes=64)
+
+        def quantise_members(g):
+            nc.vector.quantize_mx(
+                out=members_codes[:, g, :].bitcast(FP8X4),
+                scales=members_scales[:, g, :],
+                in_=members_grouped[:, g].rearrange("p c t -> p (c t)"),
+            )
+
+        def gram(s):
+            q, g = divmod(s, PASSES)
+            banks = []
+            for b in range(PACK // BANK_TILES):
+                bank = gram_psum.tile([P, BANK_TILES, GROUP], F32, tag="gram", name="gram_bank")
+                for h in range(BANK_TILES):
+                    for r in range(GROUP_TILES):
+                        row_tile = q * GROUP_TILES + r
+                        nc.tensor.matmul(
+                            out=bank[:, h, r * P : (r + 1) * P],
+                            lhsT=sq[:, row_tile : row_tile + 1].to_broadcast([P, P]),
+                            rhs=ident_f32[:],
+                            is_transpose=True,
+                            start=(h == 0 and r == 0),
+                            stop=False,
+                        )
+                banks.append(bank)
+            for b in range(PACK // BANK_TILES):
+                for h in range(BANK_TILES):
+                    a = g * PACK + b * BANK_TILES + h
+                    nc.tensor.matmul(
+                        out=banks[b][:, h, :],
+                        lhsT=featsT_m2[:, a * P : (a + 1) * P],
+                        rhs=featsT[:, q * GROUP : (q + 1) * GROUP],
+                        start=False,
+                        stop=(h == BANK_TILES - 1),
+                    )
+            return banks
+
+        def clamp_and_root(s, banks):
+            g = s % PASSES
+            d2 = work.tile([P, PACK, GROUP], F32, tag="d2")
+            for t in range(PACK):
+                b, h = divmod(t, BANK_TILES)
+                a = g * PACK + t
+                nc.vector.tensor_scalar(
+                    out=d2[:, t, :],
+                    in0=banks[b][:, h, :],
+                    scalar1=sq[:, a : a + 1],
+                    scalar2=D2_FLOOR,
+                    op0=ALU.add,
+                    op1=ALU.max,
+                )
+            dist = work.tile([P, GROUP, PACK], F32, tag="dist")
+            nc.scalar.activation(
+                out=dist[:], in_=d2[:].rearrange("p t n -> p n t"), func=ACT.Sqrt
+            )
+            return dist
+
+        def transpose_pf(s):
+            q, g = divmod(s, PASSES)
+            pfT = pft_psum.tile([P, WORDS * GROUP], F32, tag="pft")
+            for r in range(GROUP_TILES):
+                row_words = pf_sb[q][:, r, :].bitcast(F32)
+                for w in range(WORDS):
+                    first_word = g * WORDS * P + w
+                    nc.tensor.transpose(
+                        pfT[:, w * GROUP + r * P : w * GROUP + (r + 1) * P],
+                        row_words[:, first_word : (g + 1) * WORDS * P : WORDS],
+                        ident_f32[:],
+                    )
+            return pfT
+
+        def multiply(dist, pfT):
+            force = work.tile([P, GROUP * PACK], BF16, tag="force", align_bytes=64)
+            nc.vector.tensor_tensor(
+                out=force[:].rearrange("p (n w e) -> p n w e", w=WORDS, e=PAIR),
+                in0=dist[:].rearrange("p n (w e) -> p n w e", e=PAIR),
+                in1=pfT[:].bitcast(BF16).rearrange("p (w n e) -> p n w e", w=WORDS, e=PAIR),
+                op=ALU.mult,
+            )
+            return force
+
+        def quantise(force):
+            codes = work.tile([P, GROUP], U32, tag="codes", align_bytes=64)
+            scales = work.tile([P, GROUP], U8, tag="scales", align_bytes=64)
+            nc.vector.quantize_mx(out=codes[:].bitcast(FP8X4), scales=scales[:], in_=force[:])
+            return codes, scales
+
+        def multiply_members(s, codes, scales, acc):
+            q, g = divmod(s, PASSES)
+            for r in range(GROUP_TILES):
+                if g == 0:
+                    acc[r] = acc_psum.tile([P, CLUSTERS], F32, tag="acc", name="acc_bank")
+                nc.tensor.matmul_mx(
+                    out=acc[r][:],
+                    lhsT=codes[:, r * P : (r + 1) * P].bitcast(FP8X4),
+                    lhsT_scale=scales[:, r * P : (r + 1) * P],
+                    rhs=members_codes[:, g, :].bitcast(FP8X4),
+                    rhs_scale=members_scales[:, g, :],
+                    start=(g == 0),
+                    stop=(g == PASSES - 1),
+                )
+            if g == PASSES - 1:
+                for r in range(GROUP_TILES):
+                    g_row, w_row = divmod(q, WORDS)
+                    result = work.tile([P, CLUSTERS], F32, tag="result")
+                    nc.scalar.copy(out=result[:], in_=acc[r][:])
+                    nc.sync.dma_start(out=out_rows[:, g_row, w_row, r, :], in_=result[:])
+
+        gram_banks = {0: gram(0)}
+        dists = {}
+        pfTs = {}
+        acc = {}
+        for s in range(STEPS + LAG):
+            done = s - LAG
+            if done >= 0:
+                force = multiply(dists[done], pfTs[done])
+            if s + 1 < STEPS:
+                gram_banks[s + 1] = gram(s + 1)
+            if s < STEPS:
+                dists[s] = clamp_and_root(s, gram_banks[s])
+            if 0 <= done < PASSES:
+                quantise_members(done)
+            if done >= 0:
+                codes, scales = quantise(force)
+            if s < STEPS:
+                pfTs[s] = transpose_pf(s)
+            if done >= 0:
+                multiply_members(done, codes, scales, acc)

@@ -18,20 +18,15 @@ D2_FLOOR = 1e-12
 
 P = 128
 PACK = 4
-K_PASS = P * PACK
-PASSES = NODES // K_PASS
+HALF = P * PACK
+HALVES = NODES // HALF
 TILES = NODES // P
-BANK = 512
+PAIR = 2
+WORDS = PACK // PAIR
 
 GROUP_TILES = 2
 GROUP = GROUP_TILES * P
 GROUPS = NODES // GROUP
-STEPS = GROUPS * PASSES
-BANK_TILES = BANK // GROUP
-PAIR = 2
-WORDS = PACK // PAIR
-
-LAG = 2
 
 FLOPS = 2 * NODES * NODES * CODE + 2 * NODES * NODES * CLUSTERS
 
@@ -39,36 +34,52 @@ FLOPS = 2 * NODES * NODES * CODE + 2 * NODES * NODES * CLUSTERS
 def tile_controencodnet_pb_kernel(tc, feats, pf_offdiag, members, out):
     nc = tc.nc
 
-    feats_nodes = feats.rearrange("(g p w e) c -> p g w e c", g=PASSES, w=WORDS, e=PAIR)
-    pf_rows = pf_offdiag.rearrange("(g p w e) j -> p g w e j", g=PASSES, w=WORDS, e=PAIR)
-    members_nodes = members.rearrange("(g p w e) c -> p g w e c", g=PASSES, w=WORDS, e=PAIR)
-    out_rows = out.rearrange("(g p w e) c -> p g w e c", g=PASSES, w=WORDS, e=PAIR)
+    feats_nodes = feats.rearrange("(g p w e) c -> p g w e c", g=HALVES, w=WORDS, e=PAIR)
+    pf_rows = pf_offdiag.rearrange("(g p w e) j -> p g w e j", g=HALVES, w=WORDS, e=PAIR)
+    members_nodes = members.rearrange("(g p w e) c -> p g w e c", g=HALVES, w=WORDS, e=PAIR)
+    out_rows = out.rearrange("(g p w e) c -> p g w e c", g=HALVES, w=WORDS, e=PAIR)
 
     with ExitStack() as ctx:
         ctx.enter_context(tc.manual_schedule())
         keep = ctx.enter_context(tc.tile_pool(name="keep", bufs=1))
-        work = ctx.enter_context(tc.tile_pool(name="work", bufs=LAG + 1))
-        gram_psum = ctx.enter_context(tc.psum_pool(name="gram_psum", bufs=4))
-        pft_psum = ctx.enter_context(tc.psum_pool(name="pft_psum", bufs=2))
-        acc_psum = ctx.enter_context(tc.psum_pool(name="acc_psum", bufs=GROUP_TILES))
+        work = ctx.enter_context(tc.tile_pool(name="work", bufs=8))
+        psum = ctx.enter_context(tc.psum_pool(name="psum", bufs=8))
 
-        feats_sb = keep.tile([P, PASSES, PACK, CODE], BF16)
-        for g in range(PASSES):
+        feats_sb = keep.tile([P, HALVES, PACK, CODE], BF16)
+        pf_sb = {}
+        members_sb = keep.tile([P, HALVES, PACK, CLUSTERS], BF16)
+
+        def load_feats(g):
             nc.sync.dma_start(
                 out=feats_sb[:, g].rearrange("p (w e) c -> p w e c", e=PAIR), in_=feats_nodes[:, g]
             )
-        members_sb = keep.tile([P, PASSES, PACK, CLUSTERS], BF16)
-        for g in range(PASSES):
+
+        def load_pf(q, g):
+            g_row, w_row = divmod(q, WORDS)
+            pf_block = keep.tile([P, GROUP_TILES, HALF], BF16, name="pf_%d_%d" % (q, g))
+            nc.sync.dma_start(
+                out=pf_block[:], in_=pf_rows[:, g_row, w_row, :, g * HALF : (g + 1) * HALF]
+            )
+            pf_sb[q, g] = pf_block
+
+        def load_members(g):
             nc.sync.dma_start(
                 out=members_sb[:, g].rearrange("p (w e) c -> p w e c", e=PAIR),
                 in_=members_nodes[:, g],
             )
-        pf_sb = []
-        for q in range(GROUPS):
-            g_row, w_row = divmod(q, WORDS)
-            pf_group = keep.tile([P, GROUP_TILES, NODES], BF16, name="pf_group%d" % q)
-            nc.sync.dma_start(out=pf_group[:], in_=pf_rows[:, g_row, w_row])
-            pf_sb.append(pf_group)
+
+        load_feats(1)
+        load_feats(0)
+        load_members(0)
+        load_pf(0, 1)
+        load_pf(2, 0)
+        load_pf(3, 0)
+        load_pf(1, 1)
+        load_members(1)
+        load_pf(0, 0)
+        load_pf(1, 0)
+        load_pf(2, 1)
+        load_pf(3, 1)
 
         one = keep.tile([P, 1], F32)
         nc.vector.memset(one[:], 1.0)
@@ -77,22 +88,37 @@ def tile_controencodnet_pb_kernel(tc, feats, pf_offdiag, members, out):
         make_identity(nc, ident_bf16[:])
         ident_f32 = keep.tile([P, P], F32)
         make_identity(nc, ident_f32[:])
+        zero = keep.tile([P, 1], F32)
+        nc.gpsimd.memset(zero[:], 0.0)
+        floor = keep.tile([P, 1], F32)
+        nc.gpsimd.tensor_scalar(
+            out=floor[:],
+            in0=zero[:],
+            scalar1=1.0,
+            scalar2=D2_FLOOR,
+            op0=ALU.mult,
+            op1=ALU.add,
+        )
 
         featsT = keep.tile([P, NODES], BF16)
         featsT_m2 = keep.tile([P, NODES], BF16)
-        for g in range(PASSES):
-            featsT_ps = pft_psum.tile([P, K_PASS], BF16, tag="pft")
+        featsT_ps = {}
+        for g in (1, 0):
+            bank = psum.tile([P, HALF], BF16, tag="bank", name="featsT_bank")
             for t in range(PACK):
                 nc.tensor.transpose(
-                    featsT_ps[:, t * P : (t + 1) * P], feats_sb[:, g, t, :], ident_bf16[:]
+                    bank[:, t * P : (t + 1) * P], feats_sb[:, g, t, :], ident_bf16[:]
                 )
-            pass_cols = slice(g * K_PASS, (g + 1) * K_PASS)
-            nc.vector.tensor_copy(out=featsT[:, pass_cols], in_=featsT_ps[:])
-            nc.vector.tensor_scalar_mul(out=featsT_m2[:, pass_cols], in0=featsT_ps[:], scalar1=-2.0)
+            featsT_ps[g] = bank
+        half_cols = [slice(g * HALF, (g + 1) * HALF) for g in range(HALVES)]
+        nc.vector.tensor_copy(out=featsT[:, half_cols[1]], in_=featsT_ps[1][:])
+        nc.vector.tensor_scalar_mul(
+            out=featsT_m2[:, half_cols[0]], in0=featsT_ps[0][:], scalar1=-2.0
+        )
 
         squares = keep.tile([P, TILES, CODE], F32)
         sq = keep.tile([P, TILES], F32)
-        for a in range(TILES):
+        for a in (4, 5, 6, 7, 0, 1, 2, 3):
             g, t = divmod(a, PACK)
             nc.scalar.activation(
                 out=squares[:, a, :],
@@ -101,8 +127,11 @@ def tile_controencodnet_pb_kernel(tc, feats, pf_offdiag, members, out):
                 accum_out=sq[:, a : a + 1],
             )
 
-        members_grouped = keep.tile([P, PASSES, CLUSTERS, PACK], BF16, align_bytes=64)
-        for g in range(PASSES):
+        members_grouped = keep.tile([P, HALVES, CLUSTERS, PACK], BF16, align_bytes=64)
+        members_codes = keep.tile([P, HALVES, CLUSTERS], U32, align_bytes=64)
+        members_scales = keep.tile([P, HALVES, CLUSTERS], U8, align_bytes=64)
+
+        def group_members(g):
             nc.gpsimd.tensor_scalar(
                 out=members_grouped[:, g],
                 in0=members_sb[:, g].rearrange("p t c -> p c t"),
@@ -111,8 +140,6 @@ def tile_controencodnet_pb_kernel(tc, feats, pf_offdiag, members, out):
                 op0=ALU.mult,
                 op1=ALU.add,
             )
-        members_codes = keep.tile([P, PASSES, CLUSTERS], U32, align_bytes=64)
-        members_scales = keep.tile([P, PASSES, CLUSTERS], U8, align_bytes=64)
 
         def quantise_members(g):
             nc.vector.quantize_mx(
@@ -121,123 +148,250 @@ def tile_controencodnet_pb_kernel(tc, feats, pf_offdiag, members, out):
                 in_=members_grouped[:, g].rearrange("p c t -> p (c t)"),
             )
 
-        def gram(s):
-            q, g = divmod(s, PASSES)
-            banks = []
-            for b in range(PACK // BANK_TILES):
-                bank = gram_psum.tile([P, BANK_TILES, GROUP], F32, tag="gram", name="gram_bank")
-                for h in range(BANK_TILES):
-                    for r in range(GROUP_TILES):
-                        row_tile = q * GROUP_TILES + r
-                        nc.tensor.matmul(
-                            out=bank[:, h, r * P : (r + 1) * P],
-                            lhsT=sq[:, row_tile : row_tile + 1].to_broadcast([P, P]),
-                            rhs=ident_f32[:],
-                            is_transpose=True,
-                            start=(h == 0 and r == 0),
-                            stop=False,
-                        )
-                banks.append(bank)
-            for b in range(PACK // BANK_TILES):
-                for h in range(BANK_TILES):
-                    a = g * PACK + b * BANK_TILES + h
+        dist = {}
+        banks = {}
+        sq_less_floor = keep.tile([P, TILES], F32)
+        nc.gpsimd.tensor_scalar(
+            out=sq_less_floor[:],
+            in0=sq[:],
+            scalar1=1.0,
+            scalar2=-D2_FLOOR,
+            op0=ALU.mult,
+            op1=ALU.add,
+        )
+
+        def gram(panel):
+            g, h, tiles, rows = panel
+            width = len(rows) * P
+            bank = psum.tile([P, len(tiles), width], F32, tag="bank", name="gram_bank")
+            for b in range(len(tiles)):
+                for c, r in enumerate(rows):
+                    row_tile = h * PACK + r
                     nc.tensor.matmul(
-                        out=banks[b][:, h, :],
-                        lhsT=featsT_m2[:, a * P : (a + 1) * P],
-                        rhs=featsT[:, q * GROUP : (q + 1) * GROUP],
-                        start=False,
-                        stop=(h == BANK_TILES - 1),
+                        out=bank[:, b, c * P : (c + 1) * P],
+                        lhsT=sq[:, row_tile : row_tile + 1].to_broadcast([P, P]),
+                        rhs=ident_f32[:],
+                        is_transpose=True,
+                        start=(b == 0 and c == 0),
+                        stop=False,
                     )
-            return banks
-
-        def clamp_and_root(s, banks):
-            g = s % PASSES
-            d2 = work.tile([P, PACK, GROUP], F32, tag="d2")
-            for t in range(PACK):
-                b, h = divmod(t, BANK_TILES)
+            first_row = h * HALF + rows[0] * P
+            for b, t in enumerate(tiles):
                 a = g * PACK + t
-                nc.vector.tensor_scalar(
-                    out=d2[:, t, :],
-                    in0=banks[b][:, h, :],
-                    scalar1=sq[:, a : a + 1],
-                    scalar2=D2_FLOOR,
-                    op0=ALU.add,
-                    op1=ALU.max,
+                nc.tensor.matmul(
+                    out=bank[:, b, :],
+                    lhsT=featsT_m2[:, a * P : (a + 1) * P],
+                    rhs=featsT[:, first_row : first_row + width],
+                    start=False,
+                    stop=(b == len(tiles) - 1),
                 )
-            dist = work.tile([P, GROUP, PACK], F32, tag="dist")
-            nc.scalar.activation(
-                out=dist[:], in_=d2[:].rearrange("p t n -> p n t"), func=ACT.Sqrt
-            )
-            return dist
+            banks[panel] = bank
 
-        def transpose_pf(s):
-            q, g = divmod(s, PASSES)
-            pfT = pft_psum.tile([P, WORDS * GROUP], F32, tag="pft")
-            for r in range(GROUP_TILES):
-                row_words = pf_sb[q][:, r, :].bitcast(F32)
-                for w in range(WORDS):
-                    first_word = g * WORDS * P + w
-                    nc.tensor.transpose(
-                        pfT[:, w * GROUP + r * P : w * GROUP + (r + 1) * P],
-                        row_words[:, first_word : (g + 1) * WORDS * P : WORDS],
-                        ident_f32[:],
+        d2s = {}
+
+        def clamp(panel, on_scalar=False):
+            g, h, tiles, rows = panel
+            bank = banks.pop(panel)
+            d2 = work.tile([P, len(tiles), len(rows) * P], F32, tag="d2", name="d2")
+            for b, t in enumerate(tiles):
+                a = g * PACK + t
+                if on_scalar:
+                    nc.scalar.activation(
+                        out=d2[:, b, :],
+                        in_=bank[:, b, :],
+                        func=ACT.Relu,
+                        bias=sq_less_floor[:, a : a + 1],
                     )
-            return pfT
+                else:
+                    nc.vector.tensor_scalar(
+                        out=d2[:, b, :],
+                        in0=bank[:, b, :],
+                        scalar1=sq[:, a : a + 1],
+                        scalar2=D2_FLOOR,
+                        op0=ALU.add,
+                        op1=ALU.max,
+                    )
+            d2s[panel] = d2, on_scalar
 
-        def multiply(dist, pfT):
-            force = work.tile([P, GROUP * PACK], BF16, tag="force", align_bytes=64)
+        def root(panel):
+            g, h, tiles, rows = panel
+            if (g, h) not in dist:
+                dist[g, h] = keep.tile([P, PACK, HALF], F32, name="dist_%d_%d" % (g, h))
+            d2, on_scalar = d2s.pop(panel)
+            nc.scalar.activation(
+                out=dist[g, h][
+                    :, tiles[0] : tiles[-1] + 1, rows[0] * P : (rows[-1] + 1) * P
+                ],
+                in_=d2[:],
+                func=ACT.Sqrt,
+                bias=floor[:] if on_scalar else 0.0,
+            )
+
+        def transpose_words(row_words):
+            bank = psum.tile([P, WORDS, GROUP], F32, tag="bank", name="word_bank")
+            for r in range(GROUP_TILES):
+                for w in range(WORDS):
+                    nc.tensor.transpose(
+                        bank[:, w, r * P : (r + 1) * P], row_words(r)[:, w::WORDS], ident_f32[:]
+                    )
+            return bank
+
+        def transpose_pf(q, g):
+            return transpose_words(lambda r: pf_sb[q, g][:, r, :].bitcast(F32))
+
+        def multiply(q, g, pfT):
+            h, w_row = divmod(q, WORDS)
+            force = work.tile([P, GROUP * PACK], BF16, tag="force", align_bytes=64, name="force")
             nc.vector.tensor_tensor(
                 out=force[:].rearrange("p (n w e) -> p n w e", w=WORDS, e=PAIR),
-                in0=dist[:].rearrange("p n (w e) -> p n w e", e=PAIR),
-                in1=pfT[:].bitcast(BF16).rearrange("p (w n e) -> p n w e", w=WORDS, e=PAIR),
+                in0=dist[g, h][:, :, w_row * GROUP : (w_row + 1) * GROUP].rearrange(
+                    "p (w e) n -> p n w e", e=PAIR
+                ),
+                in1=pfT[:].rearrange("p w n -> p (w n)").bitcast(BF16).rearrange(
+                    "p (w n e) -> p n w e", w=WORDS, e=PAIR
+                ),
                 op=ALU.mult,
             )
             return force
 
-        def quantise(force):
-            codes = work.tile([P, GROUP], U32, tag="codes", align_bytes=64)
-            scales = work.tile([P, GROUP], U8, tag="scales", align_bytes=64)
-            nc.vector.quantize_mx(out=codes[:].bitcast(FP8X4), scales=scales[:], in_=force[:])
-            return codes, scales
+        force_rows = {}
 
-        def multiply_members(s, codes, scales, acc):
-            q, g = divmod(s, PASSES)
+        def multiply_rows(q, g, r, engine):
+            h, w_row = divmod(q, WORDS)
+            product = keep.tile([P, HALF], BF16, name="rows_%d_%d_%d" % (q, g, r))
+            engine.tensor_tensor(
+                out=product[:].rearrange("p (m u) -> p m u", u=PACK),
+                in0=dist[h, g][:, w_row * PAIR + r, :].rearrange("p (u m) -> p m u", u=PACK),
+                in1=pf_sb[q, g][:, r, :].rearrange("p (m u) -> p m u", u=PACK),
+                op=ALU.mult,
+            )
+            force_rows[q, g, r] = product
+
+        def transpose_force(q, g):
+            return transpose_words(lambda r: force_rows[q, g, r][:].bitcast(F32))
+
+        def group_force(forceT):
+            force = work.tile([P, GROUP * PACK], BF16, tag="force", align_bytes=64, name="force")
+            nc.scalar.copy(
+                out=force[:].bitcast(F32).rearrange("p (n w) -> p n w", w=WORDS),
+                in_=forceT[:].rearrange("p w n -> p n w"),
+            )
+            return force
+
+        codes = {}
+
+        def quantise(q, g, force):
+            packed = keep.tile([P, GROUP], U32, name="codes_%d_%d" % (q, g), align_bytes=64)
+            scales = keep.tile([P, GROUP], U8, name="scales_%d_%d" % (q, g), align_bytes=64)
+            nc.vector.quantize_mx(out=packed[:].bitcast(FP8X4), scales=scales[:], in_=force[:])
+            codes[q, g] = packed, scales
+
+        def multiply_members(q):
+            acc = []
             for r in range(GROUP_TILES):
-                if g == 0:
-                    acc[r] = acc_psum.tile([P, CLUSTERS], F32, tag="acc", name="acc_bank")
-                nc.tensor.matmul_mx(
-                    out=acc[r][:],
-                    lhsT=codes[:, r * P : (r + 1) * P].bitcast(FP8X4),
-                    lhsT_scale=scales[:, r * P : (r + 1) * P],
-                    rhs=members_codes[:, g, :].bitcast(FP8X4),
-                    rhs_scale=members_scales[:, g, :],
-                    start=(g == 0),
-                    stop=(g == PASSES - 1),
-                )
-            if g == PASSES - 1:
-                for r in range(GROUP_TILES):
-                    g_row, w_row = divmod(q, WORDS)
-                    result = work.tile([P, CLUSTERS], F32, tag="result")
-                    nc.scalar.copy(out=result[:], in_=acc[r][:])
-                    nc.sync.dma_start(out=out_rows[:, g_row, w_row, r, :], in_=result[:])
+                bank = psum.tile([P, CLUSTERS], F32, tag="bank", name="acc_bank")
+                for g in range(HALVES):
+                    packed, scales = codes[q, g]
+                    nc.tensor.matmul_mx(
+                        out=bank[:],
+                        lhsT=packed[:, r * P : (r + 1) * P].bitcast(FP8X4),
+                        lhsT_scale=scales[:, r * P : (r + 1) * P],
+                        rhs=members_codes[:, g, :].bitcast(FP8X4),
+                        rhs_scale=members_scales[:, g, :],
+                        start=(g == 0),
+                        stop=(g == HALVES - 1),
+                    )
+                acc.append(bank)
+            return acc
 
-        gram_banks = {0: gram(0)}
-        dists = {}
-        pfTs = {}
-        acc = {}
-        for s in range(STEPS + LAG):
-            done = s - LAG
-            if done >= 0:
-                force = multiply(dists[done], pfTs[done])
-            if s + 1 < STEPS:
-                gram_banks[s + 1] = gram(s + 1)
-            if s < STEPS:
-                dists[s] = clamp_and_root(s, gram_banks[s])
-            if 0 <= done < PASSES:
-                quantise_members(done)
-            if done >= 0:
-                codes, scales = quantise(force)
-            if s < STEPS:
-                pfTs[s] = transpose_pf(s)
-            if done >= 0:
-                multiply_members(done, codes, scales, acc)
+        def store(q, r, bank, engine_copy):
+            h, w_row = divmod(q, WORDS)
+            result = keep.tile([P, CLUSTERS], F32, name="result_%d_%d" % (q, r))
+            engine_copy(out=result[:], in_=bank[:])
+            nc.sync.dma_start(out=out_rows[:, h, w_row, r, :], in_=result[:])
+
+        full = range(PACK)
+        upper = range(GROUP_TILES, PACK)
+        p01 = [(0, 1, (t,), tuple(full)) for t in full]
+        p00 = [(0, 0, (t,), tuple(full)) for t in range(GROUP_TILES)] + [(0, 0, tuple(upper), tuple(upper))]
+        p11 = [(1, 1, (t,), tuple(full)) for t in range(GROUP_TILES)] + [(1, 1, tuple(upper), tuple(upper))]
+        gram(p01[0])
+        gram(p01[1])
+        nc.scalar.copy(out=featsT[:, half_cols[0]], in_=featsT_ps[0][:])
+        nc.scalar.mul(out=featsT_m2[:, half_cols[1]], in_=featsT_ps[1][:], mul=-2.0)
+        group_members(0)
+        gram(p01[2])
+        clamp(p01[0])
+        gram(p01[3])
+        clamp(p01[1])
+        root(p01[0])
+        clamp(p01[2])
+        root(p01[1])
+        gram(p00[0])
+        clamp(p01[3])
+        root(p01[2])
+        gram(p00[1])
+        root(p01[3])
+        multiply_rows(0, 1, 0, nc.gpsimd)
+        multiply_rows(0, 1, 1, nc.gpsimd)
+        group_members(1)
+        clamp(p00[0])
+        multiply_rows(1, 1, 0, nc.vector)
+        pfT20 = transpose_pf(2, 0)
+        gram(p00[2])
+        clamp(p00[1], True)
+        root(p00[0])
+        root(p00[1])
+        pfT30 = transpose_pf(3, 0)
+        f20 = multiply(2, 0, pfT20)
+        clamp(p00[2])
+        root(p00[2])
+        gram(p11[0])
+        gram(p11[1])
+        multiply_rows(1, 1, 1, nc.vector)
+        pfT10 = transpose_pf(1, 0)
+        f30 = multiply(3, 0, pfT30)
+        multiply_rows(0, 0, 0, nc.vector)
+        multiply_rows(0, 0, 1, nc.vector)
+        clamp(p11[0], True)
+        root(p11[0])
+        gram(p11[2])
+        clamp(p11[1], True)
+        root(p11[1])
+        fT11 = transpose_force(1, 1)
+        fT00 = transpose_force(0, 0)
+        fT01 = transpose_force(0, 1)
+        clamp(p11[2])
+        f10 = multiply(1, 0, pfT10)
+        root(p11[2])
+        f11 = group_force(fT11)
+        f00 = group_force(fT00)
+        f01 = group_force(fT01)
+        quantise_members(0)
+        quantise_members(1)
+        multiply_rows(2, 1, 0, nc.vector)
+        multiply_rows(2, 1, 1, nc.vector)
+        quantise(1, 0, f10)
+        quantise(1, 1, f11)
+        pfT31 = transpose_pf(3, 1)
+        fT21 = transpose_force(2, 1)
+        f21 = group_force(fT21)
+        acc1 = multiply_members(1)
+        f31 = multiply(3, 1, pfT31)
+        quantise(0, 0, f00)
+        quantise(0, 1, f01)
+        acc0 = multiply_members(0)
+        store(1, 0, acc1[0], nc.scalar.copy)
+        store(1, 1, acc1[1], nc.scalar.copy)
+        quantise(2, 0, f20)
+        quantise(2, 1, f21)
+        acc2 = multiply_members(2)
+        quantise(3, 0, f30)
+        quantise(3, 1, f31)
+        acc3 = multiply_members(3)
+        store(0, 0, acc0[0], nc.scalar.copy)
+        store(0, 1, acc0[1], nc.scalar.copy)
+        store(2, 0, acc2[0], nc.vector.tensor_copy)
+        store(2, 1, acc2[1], nc.scalar.copy)
+        store(3, 0, acc3[0], nc.vector.tensor_copy)
+        store(3, 1, acc3[1], nc.scalar.copy)

@@ -24,6 +24,8 @@ TILES = NODES // P
 PAIR = 2
 WORDS = PACK // PAIR
 
+RUN = 4
+
 GROUP_TILES = 2
 GROUP = GROUP_TILES * P
 GROUPS = NODES // GROUP
@@ -228,11 +230,11 @@ def tile_controencodnet_pb_kernel(tc, feats, pf_offdiag, members, out):
             )
 
         def transpose_words(row_words):
-            bank = psum.tile([P, WORDS, GROUP], F32, tag="bank", name="word_bank")
+            bank = psum.tile([P, GROUP, WORDS], F32, tag="bank", name="word_bank")
             for r in range(GROUP_TILES):
                 for w in range(WORDS):
                     nc.tensor.transpose(
-                        bank[:, w, r * P : (r + 1) * P], row_words(r)[:, w::WORDS], ident_f32[:]
+                        bank[:, r * P : (r + 1) * P, w], row_words(r)[:, w::WORDS], ident_f32[:]
                     )
             return bank
 
@@ -243,12 +245,12 @@ def tile_controencodnet_pb_kernel(tc, feats, pf_offdiag, members, out):
             h, w_row = divmod(q, WORDS)
             force = work.tile([P, GROUP * PACK], BF16, tag="force", align_bytes=64, name="force")
             nc.vector.tensor_tensor(
-                out=force[:].rearrange("p (n w e) -> p n w e", w=WORDS, e=PAIR),
+                out=force[:].rearrange("p (n i t) -> p n t i", i=RUN, t=PACK),
                 in0=dist[g, h][:, :, w_row * GROUP : (w_row + 1) * GROUP].rearrange(
-                    "p (w e) n -> p n w e", e=PAIR
+                    "p t (n i) -> p n t i", i=RUN
                 ),
-                in1=pfT[:].rearrange("p w n -> p (w n)").bitcast(BF16).rearrange(
-                    "p (w n e) -> p n w e", w=WORDS, e=PAIR
+                in1=pfT[:].rearrange("p n w -> p (n w)").bitcast(BF16).rearrange(
+                    "p (n i t) -> p n t i", i=RUN, t=PACK
                 ),
                 op=ALU.mult,
             )
@@ -260,9 +262,11 @@ def tile_controencodnet_pb_kernel(tc, feats, pf_offdiag, members, out):
             h, w_row = divmod(q, WORDS)
             product = keep.tile([P, HALF], BF16, name="rows_%d_%d_%d" % (q, g, r))
             engine.tensor_tensor(
-                out=product[:].rearrange("p (m u) -> p m u", u=PACK),
-                in0=dist[h, g][:, w_row * PAIR + r, :].rearrange("p (u m) -> p m u", u=PACK),
-                in1=pf_sb[q, g][:, r, :].rearrange("p (m u) -> p m u", u=PACK),
+                out=product[:].rearrange("p (m i u) -> p m u i", i=RUN, u=PACK),
+                in0=dist[h, g][:, w_row * PAIR + r, :].rearrange(
+                    "p (u m i) -> p m u i", u=PACK, i=RUN
+                ),
+                in1=pf_sb[q, g][:, r, :].rearrange("p (m i u) -> p m u i", i=RUN, u=PACK),
                 op=ALU.mult,
             )
             force_rows[q, g, r] = product
@@ -273,8 +277,8 @@ def tile_controencodnet_pb_kernel(tc, feats, pf_offdiag, members, out):
         def group_force(forceT):
             force = work.tile([P, GROUP * PACK], BF16, tag="force", align_bytes=64, name="force")
             nc.scalar.copy(
-                out=force[:].bitcast(F32).rearrange("p (n w) -> p n w", w=WORDS),
-                in_=forceT[:].rearrange("p w n -> p n w"),
+                out=force[:].bitcast(F32),
+                in_=forceT[:].rearrange("p n w -> p (n w)"),
             )
             return force
 

@@ -45,7 +45,8 @@ def tile_controencodnet_pb_kernel(tc, feats, pf_offdiag, members, out):
         ctx.enter_context(tc.manual_schedule())
         keep = ctx.enter_context(tc.tile_pool(name="keep", bufs=1))
         work = ctx.enter_context(tc.tile_pool(name="work", bufs=8))
-        psum = ctx.enter_context(tc.psum_pool(name="psum", bufs=8))
+        psum = ctx.enter_context(tc.psum_pool(name="psum", bufs=4))
+        acc_psum = ctx.enter_context(tc.psum_pool(name="acc_psum", bufs=4))
 
         feats_sb = keep.tile([P, HALVES, PACK, CODE], BF16)
         pf_sb = {}
@@ -290,28 +291,27 @@ def tile_controencodnet_pb_kernel(tc, feats, pf_offdiag, members, out):
             nc.vector.quantize_mx(out=packed[:].bitcast(FP8X4), scales=scales[:], in_=force[:])
             codes[q, g] = packed, scales
 
-        def multiply_members(q):
-            acc = []
-            for r in range(GROUP_TILES):
-                bank = psum.tile([P, CLUSTERS], F32, tag="bank", name="acc_bank")
-                for g in range(HALVES):
-                    packed, scales = codes[q, g]
-                    nc.tensor.matmul_mx(
-                        out=bank[:],
-                        lhsT=packed[:, r * P : (r + 1) * P].bitcast(FP8X4),
-                        lhsT_scale=scales[:, r * P : (r + 1) * P],
-                        rhs=members_codes[:, g, :].bitcast(FP8X4),
-                        rhs_scale=members_scales[:, g, :],
-                        start=(g == 0),
-                        stop=(g == HALVES - 1),
-                    )
-                acc.append(bank)
-            return acc
+        acc = {}
 
-        def store(q, r, bank, engine_copy):
+        def multiply_members(q, g, first):
+            packed, scales = codes[q, g]
+            for r in range(GROUP_TILES):
+                if first:
+                    acc[q, r] = acc_psum.tile([P, CLUSTERS], F32, tag="acc", name="acc_bank")
+                nc.tensor.matmul_mx(
+                    out=acc[q, r][:],
+                    lhsT=packed[:, r * P : (r + 1) * P].bitcast(FP8X4),
+                    lhsT_scale=scales[:, r * P : (r + 1) * P],
+                    rhs=members_codes[:, g, :].bitcast(FP8X4),
+                    rhs_scale=members_scales[:, g, :],
+                    start=first,
+                    stop=not first,
+                )
+
+        def store(q, r, engine_copy):
             h, w_row = divmod(q, WORDS)
             result = keep.tile([P, CLUSTERS], F32, name="result_%d_%d" % (q, r))
-            engine_copy(out=result[:], in_=bank[:])
+            engine_copy(out=result[:], in_=acc[q, r][:])
             nc.sync.dma_start(out=out_rows[:, h, w_row, r, :], in_=result[:])
 
         full = range(PACK)
@@ -324,6 +324,7 @@ def tile_controencodnet_pb_kernel(tc, feats, pf_offdiag, members, out):
         nc.scalar.copy(out=featsT[:, half_cols[0]], in_=featsT_ps[0][:])
         nc.scalar.mul(out=featsT_m2[:, half_cols[1]], in_=featsT_ps[1][:], mul=-2.0)
         group_members(0)
+        group_members(1)
         gram(p01[2])
         clamp(p01[0])
         gram(p01[3])
@@ -332,70 +333,73 @@ def tile_controencodnet_pb_kernel(tc, feats, pf_offdiag, members, out):
         clamp(p01[2])
         root(p01[1])
         gram(p00[0])
-        clamp(p01[3])
         root(p01[2])
-        gram(p00[1])
-        root(p01[3])
-        multiply_rows(0, 1, 0, nc.gpsimd)
-        multiply_rows(0, 1, 1, nc.gpsimd)
-        group_members(1)
-        clamp(p00[0])
-        multiply_rows(1, 1, 0, nc.vector)
-        pfT20 = transpose_pf(2, 0)
+        clamp(p01[3])
         gram(p00[2])
-        clamp(p00[1], True)
+        root(p01[3])
+        clamp(p00[0])
         root(p00[0])
-        root(p00[1])
-        pfT30 = transpose_pf(3, 0)
-        f20 = multiply(2, 0, pfT20)
+        pfT20 = transpose_pf(2, 0)
+        gram(p00[1])
         clamp(p00[2])
+        pfT30 = transpose_pf(3, 0)
+        clamp(p00[1], True)
+        root(p00[1])
         root(p00[2])
+        f20 = multiply(2, 0, pfT20)
         gram(p11[0])
-        gram(p11[1])
-        multiply_rows(1, 1, 1, nc.vector)
-        pfT10 = transpose_pf(1, 0)
         f30 = multiply(3, 0, pfT30)
-        multiply_rows(0, 0, 0, nc.vector)
-        multiply_rows(0, 0, 1, nc.vector)
         clamp(p11[0], True)
         root(p11[0])
-        gram(p11[2])
+        gram(p11[1])
+        pfT10 = transpose_pf(1, 0)
+        multiply_rows(1, 1, 0, nc.vector)
+        multiply_rows(1, 1, 1, nc.vector)
         clamp(p11[1], True)
         root(p11[1])
         fT11 = transpose_force(1, 1)
-        fT00 = transpose_force(0, 0)
-        fT01 = transpose_force(0, 1)
-        clamp(p11[2])
         f10 = multiply(1, 0, pfT10)
-        root(p11[2])
+        gram(p11[2])
         f11 = group_force(fT11)
-        f00 = group_force(fT00)
-        f01 = group_force(fT01)
+        clamp(p11[2], True)
+        root(p11[2])
         quantise_members(0)
+        quantise(3, 0, f30)
+        multiply_members(3, 0, True)
         quantise_members(1)
-        multiply_rows(2, 1, 0, nc.vector)
-        multiply_rows(2, 1, 1, nc.vector)
+        multiply_rows(0, 1, 0, nc.vector)
+        multiply_rows(0, 1, 1, nc.vector)
         quantise(1, 0, f10)
         quantise(1, 1, f11)
+        fT01 = transpose_force(0, 1)
+        multiply_members(1, 0, True)
+        multiply_members(1, 1, False)
+        f01 = group_force(fT01)
+        multiply_rows(0, 0, 0, nc.vector)
+        multiply_rows(0, 0, 1, nc.vector)
+        fT00 = transpose_force(0, 0)
+        f00 = group_force(fT00)
+        multiply_rows(2, 1, 0, nc.vector)
+        multiply_rows(2, 1, 1, nc.vector)
         pfT31 = transpose_pf(3, 1)
         fT21 = transpose_force(2, 1)
+        store(1, 0, nc.scalar.copy)
         f21 = group_force(fT21)
-        acc1 = multiply_members(1)
-        f31 = multiply(3, 1, pfT31)
-        quantise(0, 0, f00)
+        store(1, 1, nc.scalar.copy)
         quantise(0, 1, f01)
-        acc0 = multiply_members(0)
-        store(1, 0, acc1[0], nc.scalar.copy)
-        store(1, 1, acc1[1], nc.scalar.copy)
+        quantise(0, 0, f00)
+        multiply_members(0, 1, True)
+        multiply_members(0, 0, False)
+        f31 = multiply(3, 1, pfT31)
         quantise(2, 0, f20)
         quantise(2, 1, f21)
-        acc2 = multiply_members(2)
-        quantise(3, 0, f30)
+        multiply_members(2, 0, True)
+        multiply_members(2, 1, False)
+        store(0, 0, nc.scalar.copy)
+        store(0, 1, nc.scalar.copy)
         quantise(3, 1, f31)
-        acc3 = multiply_members(3)
-        store(0, 0, acc0[0], nc.scalar.copy)
-        store(0, 1, acc0[1], nc.scalar.copy)
-        store(2, 0, acc2[0], nc.vector.tensor_copy)
-        store(2, 1, acc2[1], nc.scalar.copy)
-        store(3, 0, acc3[0], nc.vector.tensor_copy)
-        store(3, 1, acc3[1], nc.scalar.copy)
+        multiply_members(3, 1, False)
+        store(2, 0, nc.vector.tensor_copy)
+        store(2, 1, nc.scalar.copy)
+        store(3, 0, nc.vector.tensor_copy)
+        store(3, 1, nc.scalar.copy)

@@ -24,6 +24,7 @@ TILES = NODES // P
 PAIR = 2
 WORDS = PACK // PAIR
 
+WARM = 4
 RUN = 4
 
 GROUP_TILES = 2
@@ -45,8 +46,7 @@ def tile_controencodnet_pb_kernel(tc, feats, pf_offdiag, members, out):
         ctx.enter_context(tc.manual_schedule())
         keep = ctx.enter_context(tc.tile_pool(name="keep", bufs=1))
         work = ctx.enter_context(tc.tile_pool(name="work", bufs=8))
-        psum = ctx.enter_context(tc.psum_pool(name="psum", bufs=4))
-        acc_psum = ctx.enter_context(tc.psum_pool(name="acc_psum", bufs=4))
+        psum = ctx.enter_context(tc.psum_pool(name="psum", bufs=8))
 
         feats_sb = keep.tile([P, HALVES, PACK, CODE], BF16)
         pf_sb = {}
@@ -84,6 +84,8 @@ def tile_controencodnet_pb_kernel(tc, feats, pf_offdiag, members, out):
         load_pf(2, 1)
         load_pf(3, 1)
 
+        zeros = keep.tile([P, HALF], BF16)
+        nc.vector.memset(zeros[:], 0.0)
         one = keep.tile([P, 1], F32)
         nc.vector.memset(one[:], 1.0)
         nc.scalar.activation(out=one[:], in_=one[:], func=ACT.Sqrt)
@@ -102,6 +104,12 @@ def tile_controencodnet_pb_kernel(tc, feats, pf_offdiag, members, out):
             op0=ALU.mult,
             op1=ALU.add,
         )
+
+        warm_bank = psum.tile([P, HALF], F32, tag="bank", name="warm_bank")
+        for k in range(WARM):
+            nc.tensor.matmul(
+                out=warm_bank[:], lhsT=zeros[:, 0:P], rhs=zeros[:], start=True, stop=True
+            )
 
         featsT = keep.tile([P, NODES], BF16)
         featsT_m2 = keep.tile([P, NODES], BF16)
@@ -150,6 +158,13 @@ def tile_controencodnet_pb_kernel(tc, feats, pf_offdiag, members, out):
                 scales=members_scales[:, g, :],
                 in_=members_grouped[:, g].rearrange("p c t -> p (c t)"),
             )
+
+        def keep_clock(count):
+            for k in range(count):
+                idle = psum.tile([P, HALF], F32, tag="bank", name="idle_bank")
+                nc.tensor.matmul(
+                    out=idle[:], lhsT=zeros[:, 0:P], rhs=zeros[:], start=True, stop=True
+                )
 
         dist = {}
         banks = {}
@@ -297,7 +312,7 @@ def tile_controencodnet_pb_kernel(tc, feats, pf_offdiag, members, out):
             packed, scales = codes[q, g]
             for r in range(GROUP_TILES):
                 if first:
-                    acc[q, r] = acc_psum.tile([P, CLUSTERS], F32, tag="acc", name="acc_bank")
+                    acc[q, r] = psum.tile([P, CLUSTERS], F32, tag="bank", name="acc_bank")
                 nc.tensor.matmul_mx(
                     out=acc[q, r][:],
                     lhsT=packed[:, r * P : (r + 1) * P].bitcast(FP8X4),
@@ -324,7 +339,6 @@ def tile_controencodnet_pb_kernel(tc, feats, pf_offdiag, members, out):
         nc.scalar.copy(out=featsT[:, half_cols[0]], in_=featsT_ps[0][:])
         nc.scalar.mul(out=featsT_m2[:, half_cols[1]], in_=featsT_ps[1][:], mul=-2.0)
         group_members(0)
-        group_members(1)
         gram(p01[2])
         clamp(p01[0])
         gram(p01[3])
@@ -334,51 +348,54 @@ def tile_controencodnet_pb_kernel(tc, feats, pf_offdiag, members, out):
         root(p01[1])
         gram(p00[0])
         root(p01[2])
+        multiply_rows(1, 1, 0, nc.gpsimd)
         clamp(p01[3])
         gram(p00[2])
         root(p01[3])
+        multiply_rows(1, 1, 1, nc.gpsimd)
+        group_members(1)
         clamp(p00[0])
         root(p00[0])
         pfT20 = transpose_pf(2, 0)
         gram(p00[1])
         clamp(p00[2])
         pfT30 = transpose_pf(3, 0)
+        keep_clock(1)
         clamp(p00[1], True)
-        root(p00[1])
         root(p00[2])
+        root(p00[1])
         f20 = multiply(2, 0, pfT20)
         gram(p11[0])
-        f30 = multiply(3, 0, pfT30)
-        clamp(p11[0], True)
-        root(p11[0])
-        gram(p11[1])
         pfT10 = transpose_pf(1, 0)
-        multiply_rows(1, 1, 0, nc.vector)
-        multiply_rows(1, 1, 1, nc.vector)
-        clamp(p11[1], True)
-        root(p11[1])
-        fT11 = transpose_force(1, 1)
+        f30 = multiply(3, 0, pfT30)
+        gram(p11[1])
+        clamp(p11[0])
+        root(p11[0])
         f10 = multiply(1, 0, pfT10)
+        clamp(p11[1], True)
+        fT11 = transpose_force(1, 1)
         gram(p11[2])
         f11 = group_force(fT11)
-        clamp(p11[2], True)
-        root(p11[2])
-        quantise_members(0)
-        quantise(3, 0, f30)
-        multiply_members(3, 0, True)
-        quantise_members(1)
+        root(p11[1])
+        keep_clock(1)
         multiply_rows(0, 1, 0, nc.vector)
         multiply_rows(0, 1, 1, nc.vector)
+        clamp(p11[2], True)
+        fT01 = transpose_force(0, 1)
+        f01 = group_force(fT01)
+        root(p11[2])
+        quantise_members(0)
+        quantise_members(1)
         quantise(1, 0, f10)
         quantise(1, 1, f11)
-        fT01 = transpose_force(0, 1)
+        keep_clock(1)
         multiply_members(1, 0, True)
         multiply_members(1, 1, False)
-        f01 = group_force(fT01)
         multiply_rows(0, 0, 0, nc.vector)
         multiply_rows(0, 0, 1, nc.vector)
         fT00 = transpose_force(0, 0)
         f00 = group_force(fT00)
+        keep_clock(1)
         multiply_rows(2, 1, 0, nc.vector)
         multiply_rows(2, 1, 1, nc.vector)
         pfT31 = transpose_pf(3, 1)
@@ -387,9 +404,11 @@ def tile_controencodnet_pb_kernel(tc, feats, pf_offdiag, members, out):
         f21 = group_force(fT21)
         store(1, 1, nc.scalar.copy)
         quantise(0, 1, f01)
+        quantise(3, 0, f30)
         quantise(0, 0, f00)
         multiply_members(0, 1, True)
         multiply_members(0, 0, False)
+        multiply_members(3, 0, True)
         f31 = multiply(3, 1, pfT31)
         quantise(2, 0, f20)
         quantise(2, 1, f21)

@@ -24,7 +24,8 @@ TILES = NODES // P
 PAIR = 2
 WORDS = PACK // PAIR
 
-WARM = 4
+WARM = 6
+IDLE = 256
 RUN = 4
 
 GROUP_TILES = 2
@@ -84,8 +85,8 @@ def tile_controencodnet_pb_kernel(tc, feats, pf_offdiag, members, out):
         load_pf(2, 1)
         load_pf(3, 1)
 
-        zeros = keep.tile([P, HALF], BF16)
-        nc.vector.memset(zeros[:], 0.0)
+        zeros = keep.tile([P, IDLE], BF16)
+        nc.vector.memset(zeros[:].bitcast(U32), 0)
         one = keep.tile([P, 1], F32)
         nc.vector.memset(one[:], 1.0)
         nc.scalar.activation(out=one[:], in_=one[:], func=ACT.Sqrt)
@@ -105,7 +106,7 @@ def tile_controencodnet_pb_kernel(tc, feats, pf_offdiag, members, out):
             op1=ALU.add,
         )
 
-        warm_bank = psum.tile([P, HALF], F32, tag="bank", name="warm_bank")
+        warm_bank = psum.tile([P, IDLE], F32, tag="bank", name="warm_bank")
         for k in range(WARM):
             nc.tensor.matmul(
                 out=warm_bank[:], lhsT=zeros[:, 0:P], rhs=zeros[:], start=True, stop=True
@@ -113,19 +114,23 @@ def tile_controencodnet_pb_kernel(tc, feats, pf_offdiag, members, out):
 
         featsT = keep.tile([P, NODES], BF16)
         featsT_m2 = keep.tile([P, NODES], BF16)
-        featsT_ps = {}
-        for g in (1, 0):
-            bank = psum.tile([P, HALF], BF16, tag="bank", name="featsT_bank")
-            for t in range(PACK):
-                nc.tensor.transpose(
-                    bank[:, t * P : (t + 1) * P], feats_sb[:, g, t, :], ident_bf16[:]
-                )
-            featsT_ps[g] = bank
         half_cols = [slice(g * HALF, (g + 1) * HALF) for g in range(HALVES)]
-        nc.vector.tensor_copy(out=featsT[:, half_cols[1]], in_=featsT_ps[1][:])
-        nc.vector.tensor_scalar_mul(
-            out=featsT_m2[:, half_cols[0]], in0=featsT_ps[0][:], scalar1=-2.0
-        )
+
+        def transpose_feats(first, count):
+            bank = psum.tile([P, count * P], BF16, tag="bank", name="featsT_bank")
+            for k in range(count):
+                g, t = divmod(first + k, PACK)
+                nc.tensor.transpose(
+                    bank[:, k * P : (k + 1) * P], feats_sb[:, g, t, :], ident_bf16[:]
+                )
+            return bank
+
+        featsT_1 = transpose_feats(PACK, PACK)
+        featsT_0a = transpose_feats(0, 1)
+        featsT_0b = transpose_feats(1, PACK - 1)
+        nc.vector.tensor_copy(out=featsT[:, half_cols[1]], in_=featsT_1[:])
+        nc.vector.tensor_scalar_mul(out=featsT_m2[:, 0:P], in0=featsT_0a[:], scalar1=-2.0)
+        nc.vector.tensor_scalar_mul(out=featsT_m2[:, P:HALF], in0=featsT_0b[:], scalar1=-2.0)
 
         squares = keep.tile([P, TILES, CODE], F32)
         sq = keep.tile([P, TILES], F32)
@@ -159,12 +164,11 @@ def tile_controencodnet_pb_kernel(tc, feats, pf_offdiag, members, out):
                 in_=members_grouped[:, g].rearrange("p c t -> p (c t)"),
             )
 
-        def keep_clock(count):
-            for k in range(count):
-                idle = psum.tile([P, HALF], F32, tag="bank", name="idle_bank")
-                nc.tensor.matmul(
-                    out=idle[:], lhsT=zeros[:, 0:P], rhs=zeros[:], start=True, stop=True
-                )
+        def keep_clock(operand):
+            idle = psum.tile([P, HALF], F32, tag="bank", name="idle_bank")
+            nc.tensor.matmul(
+                out=idle[:], lhsT=operand[:, 0:P], rhs=operand[:, 0:HALF], start=True, stop=True
+            )
 
         dist = {}
         banks = {}
@@ -336,8 +340,9 @@ def tile_controencodnet_pb_kernel(tc, feats, pf_offdiag, members, out):
         p11 = [(1, 1, (t,), tuple(full)) for t in range(GROUP_TILES)] + [(1, 1, tuple(upper), tuple(upper))]
         gram(p01[0])
         gram(p01[1])
-        nc.scalar.copy(out=featsT[:, half_cols[0]], in_=featsT_ps[0][:])
-        nc.scalar.mul(out=featsT_m2[:, half_cols[1]], in_=featsT_ps[1][:], mul=-2.0)
+        nc.scalar.copy(out=featsT[:, 0:P], in_=featsT_0a[:])
+        nc.scalar.copy(out=featsT[:, P:HALF], in_=featsT_0b[:])
+        nc.scalar.mul(out=featsT_m2[:, half_cols[1]], in_=featsT_1[:], mul=-2.0)
         group_members(0)
         gram(p01[2])
         clamp(p01[0])
@@ -348,77 +353,77 @@ def tile_controencodnet_pb_kernel(tc, feats, pf_offdiag, members, out):
         root(p01[1])
         gram(p00[0])
         root(p01[2])
-        multiply_rows(1, 1, 0, nc.gpsimd)
+        multiply_rows(0, 1, 0, nc.gpsimd)
         clamp(p01[3])
         gram(p00[2])
         root(p01[3])
-        multiply_rows(1, 1, 1, nc.gpsimd)
+        multiply_rows(0, 1, 1, nc.gpsimd)
         group_members(1)
         clamp(p00[0])
         root(p00[0])
         pfT20 = transpose_pf(2, 0)
-        gram(p00[1])
         clamp(p00[2])
+        gram(p00[1])
         pfT30 = transpose_pf(3, 0)
-        keep_clock(1)
-        clamp(p00[1], True)
+        keep_clock(featsT)
         root(p00[2])
+        clamp(p00[1], True)
         root(p00[1])
         f20 = multiply(2, 0, pfT20)
         gram(p11[0])
-        pfT10 = transpose_pf(1, 0)
         f30 = multiply(3, 0, pfT30)
         gram(p11[1])
         clamp(p11[0])
         root(p11[0])
-        f10 = multiply(1, 0, pfT10)
-        clamp(p11[1], True)
-        fT11 = transpose_force(1, 1)
+        pfT10 = transpose_pf(1, 0)
         gram(p11[2])
-        f11 = group_force(fT11)
+        clamp(p11[1], True)
         root(p11[1])
-        keep_clock(1)
-        multiply_rows(0, 1, 0, nc.vector)
-        multiply_rows(0, 1, 1, nc.vector)
-        clamp(p11[2], True)
         fT01 = transpose_force(0, 1)
+        keep_clock(featsT)
+        f10 = multiply(1, 0, pfT10)
+        clamp(p11[2], True)
         f01 = group_force(fT01)
         root(p11[2])
+        multiply_rows(1, 1, 0, nc.vector)
+        multiply_rows(1, 1, 1, nc.vector)
+        keep_clock(f10)
+        keep_clock(force_rows[1, 1, 0])
+        fT11 = transpose_force(1, 1)
+        f11 = group_force(fT11)
+        pfT31 = transpose_pf(3, 1)
         quantise_members(0)
-        quantise_members(1)
         quantise(1, 0, f10)
-        quantise(1, 1, f11)
-        keep_clock(1)
+        quantise(2, 0, f20)
         multiply_members(1, 0, True)
-        multiply_members(1, 1, False)
-        multiply_rows(0, 0, 0, nc.vector)
-        multiply_rows(0, 0, 1, nc.vector)
-        fT00 = transpose_force(0, 0)
-        f00 = group_force(fT00)
-        keep_clock(1)
+        multiply_members(2, 0, True)
         multiply_rows(2, 1, 0, nc.vector)
         multiply_rows(2, 1, 1, nc.vector)
-        pfT31 = transpose_pf(3, 1)
         fT21 = transpose_force(2, 1)
-        store(1, 0, nc.scalar.copy)
         f21 = group_force(fT21)
-        store(1, 1, nc.scalar.copy)
+        quantise_members(1)
+        quantise(1, 1, f11)
         quantise(0, 1, f01)
-        quantise(3, 0, f30)
-        quantise(0, 0, f00)
+        multiply_members(1, 1, False)
         multiply_members(0, 1, True)
-        multiply_members(0, 0, False)
+        multiply_rows(0, 0, 0, nc.vector)
+        multiply_rows(0, 0, 1, nc.vector)
+        store(1, 0, nc.scalar.copy)
+        store(1, 1, nc.scalar.copy)
+        quantise(2, 1, f21)
+        fT00 = transpose_force(0, 0)
+        f00 = group_force(fT00)
+        multiply_members(2, 1, False)
+        quantise(3, 0, f30)
         multiply_members(3, 0, True)
         f31 = multiply(3, 1, pfT31)
-        quantise(2, 0, f20)
-        quantise(2, 1, f21)
-        multiply_members(2, 0, True)
-        multiply_members(2, 1, False)
-        store(0, 0, nc.scalar.copy)
-        store(0, 1, nc.scalar.copy)
+        store(2, 0, nc.scalar.copy)
+        store(2, 1, nc.scalar.copy)
+        quantise(0, 0, f00)
+        multiply_members(0, 0, False)
         quantise(3, 1, f31)
         multiply_members(3, 1, False)
-        store(2, 0, nc.vector.tensor_copy)
-        store(2, 1, nc.scalar.copy)
+        store(0, 0, nc.vector.tensor_copy)
+        store(0, 1, nc.scalar.copy)
         store(3, 0, nc.vector.tensor_copy)
         store(3, 1, nc.scalar.copy)

@@ -173,14 +173,17 @@ def tile_controencodnet_pb_kernel(tc, feats, pf_offdiag, members, out):
         dist = {}
         banks = {}
         sq_less_floor = keep.tile([P, TILES], F32)
-        nc.gpsimd.tensor_scalar(
-            out=sq_less_floor[:],
-            in0=sq[:],
-            scalar1=1.0,
-            scalar2=-D2_FLOOR,
-            op0=ALU.mult,
-            op1=ALU.add,
-        )
+
+        def subtract_floor():
+            nc.gpsimd.tensor_scalar(
+                out=sq_less_floor[:],
+                in0=sq[:],
+                scalar1=1.0,
+                scalar2=-D2_FLOOR,
+                op0=ALU.mult,
+                op1=ALU.add,
+            )
+
 
         def gram(panel):
             g, h, tiles, rows = panel
@@ -261,15 +264,19 @@ def tile_controencodnet_pb_kernel(tc, feats, pf_offdiag, members, out):
         def transpose_pf(q, g):
             return transpose_words(lambda r: pf_sb[q, g][:, r, :].bitcast(F32))
 
-        def multiply(q, g, pfT):
+        def new_force():
+            return work.tile([P, GROUP * PACK], BF16, tag="force", align_bytes=64, name="force")
+
+        def multiply(q, g, pfT, force, row_tiles=range(GROUP_TILES)):
             h, w_row = divmod(q, WORDS)
-            force = work.tile([P, GROUP * PACK], BF16, tag="force", align_bytes=64, name="force")
+            rows = slice(row_tiles[0] * P, (row_tiles[-1] + 1) * P)
+            cols = slice(w_row * GROUP + rows.start, w_row * GROUP + rows.stop)
             nc.vector.tensor_tensor(
-                out=force[:].rearrange("p (n i t) -> p n t i", i=RUN, t=PACK),
-                in0=dist[g, h][:, :, w_row * GROUP : (w_row + 1) * GROUP].rearrange(
-                    "p t (n i) -> p n t i", i=RUN
+                out=force[:, rows.start * PACK : rows.stop * PACK].rearrange(
+                    "p (n i t) -> p n t i", i=RUN, t=PACK
                 ),
-                in1=pfT[:].rearrange("p n w -> p (n w)").bitcast(BF16).rearrange(
+                in0=dist[g, h][:, :, cols].rearrange("p t (n i) -> p n t i", i=RUN),
+                in1=pfT[:, rows, :].rearrange("p n w -> p (n w)").bitcast(BF16).rearrange(
                     "p (n i t) -> p n t i", i=RUN, t=PACK
                 ),
                 op=ALU.mult,
@@ -344,6 +351,7 @@ def tile_controencodnet_pb_kernel(tc, feats, pf_offdiag, members, out):
         nc.scalar.copy(out=featsT[:, P:HALF], in_=featsT_0b[:])
         nc.scalar.mul(out=featsT_m2[:, half_cols[1]], in_=featsT_1[:], mul=-2.0)
         group_members(0)
+        subtract_floor()
         gram(p01[2])
         clamp(p01[0])
         gram(p01[3])
@@ -369,29 +377,28 @@ def tile_controencodnet_pb_kernel(tc, feats, pf_offdiag, members, out):
         root(p00[2])
         clamp(p00[1], True)
         root(p00[1])
-        f20 = multiply(2, 0, pfT20)
+        f20 = multiply(2, 0, pfT20, new_force())
         gram(p11[0])
-        f30 = multiply(3, 0, pfT30)
+        f30 = multiply(3, 0, pfT30, new_force())
+        pfT10 = transpose_pf(1, 0)
         gram(p11[1])
         clamp(p11[0])
         root(p11[0])
-        pfT10 = transpose_pf(1, 0)
         gram(p11[2])
         clamp(p11[1], True)
-        root(p11[1])
         fT01 = transpose_force(0, 1)
-        keep_clock(featsT)
-        f10 = multiply(1, 0, pfT10)
-        clamp(p11[2], True)
         f01 = group_force(fT01)
-        root(p11[2])
+        root(p11[1])
+        keep_clock(featsT)
+        f10 = multiply(1, 0, pfT10, new_force())
+        clamp(p11[2], True)
         multiply_rows(1, 1, 0, nc.vector)
         multiply_rows(1, 1, 1, nc.vector)
         keep_clock(f10)
         keep_clock(force_rows[1, 1, 0])
         fT11 = transpose_force(1, 1)
         f11 = group_force(fT11)
-        pfT31 = transpose_pf(3, 1)
+        root(p11[2])
         quantise_members(0)
         quantise(1, 0, f10)
         quantise(2, 0, f20)
@@ -401,29 +408,30 @@ def tile_controencodnet_pb_kernel(tc, feats, pf_offdiag, members, out):
         multiply_rows(2, 1, 1, nc.vector)
         fT21 = transpose_force(2, 1)
         f21 = group_force(fT21)
+        pfT31 = transpose_pf(3, 1)
         quantise_members(1)
         quantise(1, 1, f11)
-        quantise(0, 1, f01)
         multiply_members(1, 1, False)
-        multiply_members(0, 1, True)
         multiply_rows(0, 0, 0, nc.vector)
         multiply_rows(0, 0, 1, nc.vector)
+        fT00 = transpose_force(0, 0)
         store(1, 0, nc.scalar.copy)
         store(1, 1, nc.scalar.copy)
-        quantise(2, 1, f21)
-        fT00 = transpose_force(0, 0)
         f00 = group_force(fT00)
+        quantise(2, 1, f21)
         multiply_members(2, 1, False)
+        quantise(0, 1, f01)
         quantise(3, 0, f30)
+        multiply_members(0, 1, True)
         multiply_members(3, 0, True)
-        f31 = multiply(3, 1, pfT31)
+        f31 = multiply(3, 1, pfT31, new_force())
         store(2, 0, nc.scalar.copy)
         store(2, 1, nc.scalar.copy)
         quantise(0, 0, f00)
         multiply_members(0, 0, False)
         quantise(3, 1, f31)
         multiply_members(3, 1, False)
-        store(0, 0, nc.vector.tensor_copy)
-        store(0, 1, nc.scalar.copy)
-        store(3, 0, nc.vector.tensor_copy)
-        store(3, 1, nc.scalar.copy)
+        store(0, 0, nc.scalar.copy)
+        store(0, 1, nc.vector.tensor_copy)
+        store(3, 0, nc.scalar.copy)
+        store(3, 1, nc.vector.tensor_copy)

@@ -93,7 +93,7 @@ def tile_controencodnet_pb_kernel(tc, feats, pf_offdiag, members, out):
         ident_bf16 = keep.tile([P, P], BF16)
         make_identity(nc, ident_bf16[:])
         ident_f32 = keep.tile([P, P], F32)
-        make_identity(nc, ident_f32[:])
+        nc.vector.tensor_copy(out=ident_f32[:], in_=ident_bf16[:])
         zero = keep.tile([P, 1], F32)
         nc.gpsimd.memset(zero[:], 0.0)
         floor = keep.tile([P, 1], F32)
@@ -311,11 +311,19 @@ def tile_controencodnet_pb_kernel(tc, feats, pf_offdiag, members, out):
 
         codes = {}
 
-        def quantise(q, g, force):
-            packed = keep.tile([P, GROUP], U32, name="codes_%d_%d" % (q, g), align_bytes=64)
-            scales = keep.tile([P, GROUP], U8, name="scales_%d_%d" % (q, g), align_bytes=64)
-            nc.vector.quantize_mx(out=packed[:].bitcast(FP8X4), scales=scales[:], in_=force[:])
-            codes[q, g] = packed, scales
+        def quantise(q, g, force, row_tiles=range(GROUP_TILES)):
+            if (q, g) not in codes:
+                codes[q, g] = (
+                    keep.tile([P, GROUP], U32, name="codes_%d_%d" % (q, g), align_bytes=64),
+                    keep.tile([P, GROUP], U8, name="scales_%d_%d" % (q, g), align_bytes=64),
+                )
+            packed, scales = codes[q, g]
+            rows = slice(row_tiles[0] * P, (row_tiles[-1] + 1) * P)
+            nc.vector.quantize_mx(
+                out=packed[:, rows].bitcast(FP8X4),
+                scales=scales[:, rows],
+                in_=force[:, rows.start * PACK : rows.stop * PACK],
+            )
 
         acc = {}
 
@@ -378,11 +386,11 @@ def tile_controencodnet_pb_kernel(tc, feats, pf_offdiag, members, out):
         clamp(p00[1], True)
         root(p00[1])
         f20 = multiply(2, 0, pfT20, new_force())
+        pfT10 = transpose_pf(1, 0)
         gram(p11[0])
         f30 = multiply(3, 0, pfT30, new_force())
-        pfT10 = transpose_pf(1, 0)
         gram(p11[1])
-        clamp(p11[0])
+        clamp(p11[0], True)
         root(p11[0])
         gram(p11[2])
         clamp(p11[1], True)
@@ -424,12 +432,15 @@ def tile_controencodnet_pb_kernel(tc, feats, pf_offdiag, members, out):
         quantise(3, 0, f30)
         multiply_members(0, 1, True)
         multiply_members(3, 0, True)
-        f31 = multiply(3, 1, pfT31, new_force())
+        f31 = new_force()
+        multiply(3, 1, pfT31, f31, (0,))
         store(2, 0, nc.scalar.copy)
         store(2, 1, nc.scalar.copy)
         quantise(0, 0, f00)
         multiply_members(0, 0, False)
-        quantise(3, 1, f31)
+        multiply(3, 1, pfT31, f31, (1,))
+        quantise(3, 1, f31, (0,))
+        quantise(3, 1, f31, (1,))
         multiply_members(3, 1, False)
         store(0, 0, nc.scalar.copy)
         store(0, 1, nc.vector.tensor_copy)

@@ -77,12 +77,12 @@ def tile_controencodnet_pb_kernel(tc, feats, pf_offdiag, members, out):
         load_members(0)
         load_pf(0, 1)
         load_pf(2, 0)
-        load_pf(3, 0)
-        load_pf(1, 1)
         load_members(1)
-        load_pf(0, 0)
+        load_pf(3, 0)
         load_pf(1, 0)
+        load_pf(1, 1)
         load_pf(2, 1)
+        load_pf(0, 0)
         load_pf(3, 1)
 
         zeros = keep.tile([P, IDLE], BF16)
@@ -373,7 +373,6 @@ def tile_controencodnet_pb_kernel(tc, feats, pf_offdiag, members, out):
         clamp(p01[3])
         gram(p00[2])
         root(p01[3])
-        multiply_rows(0, 1, 1, nc.gpsimd)
         group_members(1)
         clamp(p00[0])
         root(p00[0])
@@ -394,19 +393,20 @@ def tile_controencodnet_pb_kernel(tc, feats, pf_offdiag, members, out):
         root(p11[0])
         gram(p11[2])
         clamp(p11[1], True)
-        fT01 = transpose_force(0, 1)
-        f01 = group_force(fT01)
         root(p11[1])
         keep_clock(featsT)
         f10 = multiply(1, 0, pfT10, new_force())
         clamp(p11[2], True)
+        multiply_rows(0, 1, 1, nc.vector)
         multiply_rows(1, 1, 0, nc.vector)
         multiply_rows(1, 1, 1, nc.vector)
         keep_clock(f10)
+        fT01 = transpose_force(0, 1)
+        f01 = group_force(fT01)
         keep_clock(force_rows[1, 1, 0])
         fT11 = transpose_force(1, 1)
-        f11 = group_force(fT11)
         root(p11[2])
+        f11 = group_force(fT11)
         quantise_members(0)
         quantise(1, 0, f10)
         quantise(2, 0, f20)

from contextlib import ExitStack

import concourse.mybir as mybir
from concourse.masks import make_identity

F32 = mybir.dt.float32
BF16 = mybir.dt.bfloat16
U32 = mybir.dt.uint32
U8 = mybir.dt.uint8
FP8X4 = mybir.dt.float8_e4m3fn_x4
ALU = mybir.AluOpType
ACT = mybir.ActivationFunctionType

NODES = 1024
CODE = 128
CLUSTERS = 512
D2_FLOOR = 1e-12

P = 128
PACK = 4
HALF = P * PACK
HALVES = NODES // HALF
TILES = NODES // P
PAIR = 2
WORDS = PACK // PAIR

WARM = 6
IDLE = 256
RUN = 4

GROUP_TILES = 2
GROUP = GROUP_TILES * P
GROUPS = NODES // GROUP

FLOPS = 2 * NODES * NODES * CODE + 2 * NODES * NODES * CLUSTERS


def tile_controencodnet_pb_kernel(tc, feats, pf_offdiag, members, out):
    nc = tc.nc

    feats_nodes = feats.rearrange("(g p w e) c -> p g w e c", g=HALVES, w=WORDS, e=PAIR)
    pf_rows = pf_offdiag.rearrange("(g p w e) j -> p g w e j", g=HALVES, w=WORDS, e=PAIR)
    members_nodes = members.rearrange("(g p w e) c -> p g w e c", g=HALVES, w=WORDS, e=PAIR)
    out_rows = out.rearrange("(g p w e) c -> p g w e c", g=HALVES, w=WORDS, e=PAIR)

    with ExitStack() as ctx:
        ctx.enter_context(tc.manual_schedule())
        keep = ctx.enter_context(tc.tile_pool(name="keep", bufs=1))
        work = ctx.enter_context(tc.tile_pool(name="work", bufs=8))
        psum = ctx.enter_context(tc.psum_pool(name="psum", bufs=8))

        feats_sb = keep.tile([P, HALVES, PACK, CODE], BF16)
        pf_sb = {}
        members_sb = keep.tile([P, HALVES, PACK, CLUSTERS], BF16)

        def load_feats(g):
            nc.sync.dma_start(
                out=feats_sb[:, g].rearrange("p (w e) c -> p w e c", e=PAIR), in_=feats_nodes[:, g]
            )

        def load_pf(q, g):
            g_row, w_row = divmod(q, WORDS)
            pf_block = keep.tile([P, GROUP_TILES, HALF], BF16, name="pf_%d_%d" % (q, g))
            nc.sync.dma_start(
                out=pf_block[:], in_=pf_rows[:, g_row, w_row, :, g * HALF : (g + 1) * HALF]
            )
            pf_sb[q, g] = pf_block

        def load_members(g):
            nc.sync.dma_start(
                out=members_sb[:, g].rearrange("p (w e) c -> p w e c", e=PAIR),
                in_=members_nodes[:, g],
            )

        load_feats(1)
        load_feats(0)
        load_members(0)
        load_pf(0, 1)
        load_pf(2, 0)
        load_members(1)
        load_pf(3, 0)
        load_pf(1, 0)
        load_pf(1, 1)
        load_pf(2, 1)
        load_pf(0, 0)
        load_pf(3, 1)

        zeros = keep.tile([P, IDLE], BF16)
        nc.vector.memset(zeros[:].bitcast(U32), 0)
        one = keep.tile([P, 1], F32)
        nc.vector.memset(one[:], 1.0)
        nc.scalar.activation(out=one[:], in_=one[:], func=ACT.Sqrt)
        ident_bf16 = keep.tile([P, P], BF16)
        make_identity(nc, ident_bf16[:])
        ident_f32 = keep.tile([P, P], F32)
        nc.vector.tensor_copy(out=ident_f32[:], in_=ident_bf16[:])
        zero = keep.tile([P, 1], F32)
        nc.gpsimd.memset(zero[:], 0.0)
        floor = keep.tile([P, 1], F32)
        nc.gpsimd.tensor_scalar(
            out=floor[:],
            in0=zero[:],
            scalar1=1.0,
            scalar2=D2_FLOOR,
            op0=ALU.mult,
            op1=ALU.add,
        )

        warm_bank = psum.tile([P, IDLE], F32, tag="bank", name="warm_bank")
        for k in range(WARM):
            nc.tensor.matmul(
                out=warm_bank[:], lhsT=zeros[:, 0:P], rhs=zeros[:], start=True, stop=True
            )

        featsT = keep.tile([P, NODES], BF16)
        featsT_m2 = keep.tile([P, NODES], BF16)
        half_cols = [slice(g * HALF, (g + 1) * HALF) for g in range(HALVES)]

        def transpose_feats(first, count):
            bank = psum.tile([P, count * P], BF16, tag="bank", name="featsT_bank")
            for k in range(count):
                g, t = divmod(first + k, PACK)
                nc.tensor.transpose(
                    bank[:, k * P : (k + 1) * P], feats_sb[:, g, t, :], ident_bf16[:]
                )
            return bank

        featsT_1 = transpose_feats(PACK, PACK)
        featsT_0a = transpose_feats(0, 1)
        featsT_0b = transpose_feats(1, PACK - 1)
        nc.vector.tensor_copy(out=featsT[:, half_cols[1]], in_=featsT_1[:])
        nc.vector.tensor_scalar_mul(out=featsT_m2[:, 0:P], in0=featsT_0a[:], scalar1=-2.0)
        nc.vector.tensor_scalar_mul(out=featsT_m2[:, P:HALF], in0=featsT_0b[:], scalar1=-2.0)

        squares = keep.tile([P, TILES, CODE], F32)
        sq = keep.tile([P, TILES], F32)
        for a in (4, 5, 6, 7, 0, 1, 2, 3):
            g, t = divmod(a, PACK)
            nc.scalar.activation(
                out=squares[:, a, :],
                in_=feats_sb[:, g, t, :],
                func=ACT.Square,
                accum_out=sq[:, a : a + 1],
            )

        members_grouped = keep.tile([P, HALVES, CLUSTERS, PACK], BF16, align_bytes=64)
        members_codes = keep.tile([P, HALVES, CLUSTERS], U32, align_bytes=64)
        members_scales = keep.tile([P, HALVES, CLUSTERS], U8, align_bytes=64)

        def group_members(g):
            nc.gpsimd.tensor_scalar(
                out=members_grouped[:, g],
                in0=members_sb[:, g].rearrange("p t c -> p c t"),
                scalar1=1.0,
                scalar2=0.0,
                op0=ALU.mult,
                op1=ALU.add,
            )

        def quantise_members(g):
            nc.vector.quantize_mx(
                out=members_codes[:, g, :].bitcast(FP8X4),
                scales=members_scales[:, g, :],
                in_=members_grouped[:, g].rearrange("p c t -> p (c t)"),
            )

        def keep_clock(operand):
            idle = psum.tile([P, HALF], F32, tag="bank", name="idle_bank")
            nc.tensor.matmul(
                out=idle[:], lhsT=operand[:, 0:P], rhs=operand[:, 0:HALF], start=True, stop=True
            )

        dist = {}
        banks = {}
        sq_less_floor = keep.tile([P, TILES], F32)

        def subtract_floor():
            nc.gpsimd.tensor_scalar(
                out=sq_less_floor[:],
                in0=sq[:],
                scalar1=1.0,
                scalar2=-D2_FLOOR,
                op0=ALU.mult,
                op1=ALU.add,
            )


        def gram(panel):
            g, h, tiles, rows = panel
            width = len(rows) * P
            bank = psum.tile([P, len(tiles), width], F32, tag="bank", name="gram_bank")
            for b in range(len(tiles)):
                for c, r in enumerate(rows):
                    row_tile = h * PACK + r
                    nc.tensor.matmul(
                        out=bank[:, b, c * P : (c + 1) * P],
                        lhsT=sq[:, row_tile : row_tile + 1].to_broadcast([P, P]),
                        rhs=ident_f32[:],
                        is_transpose=True,
                        start=(b == 0 and c == 0),
                        stop=False,
                    )
            first_row = h * HALF + rows[0] * P
            for b, t in enumerate(tiles):
                a = g * PACK + t
                nc.tensor.matmul(
                    out=bank[:, b, :],
                    lhsT=featsT_m2[:, a * P : (a + 1) * P],
                    rhs=featsT[:, first_row : first_row + width],
                    start=False,
                    stop=(b == len(tiles) - 1),
                )
            banks[panel] = bank

        d2s = {}

        def clamp(panel, on_scalar=False):
            g, h, tiles, rows = panel
            bank = banks.pop(panel)
            d2 = work.tile([P, len(tiles), len(rows) * P], F32, tag="d2", name="d2")
            for b, t in enumerate(tiles):
                a = g * PACK + t
                if on_scalar:
                    nc.scalar.activation(
                        out=d2[:, b, :],
                        in_=bank[:, b, :],
                        func=ACT.Relu,
                        bias=sq_less_floor[:, a : a + 1],
                    )
                else:
                    nc.vector.tensor_scalar(
                        out=d2[:, b, :],
                        in0=bank[:, b, :],
                        scalar1=sq[:, a : a + 1],
                        scalar2=D2_FLOOR,
                        op0=ALU.add,
                        op1=ALU.max,
                    )
            d2s[panel] = d2, on_scalar

        def root(panel):
            g, h, tiles, rows = panel
            if (g, h) not in dist:
                dist[g, h] = keep.tile([P, PACK, HALF], F32, name="dist_%d_%d" % (g, h))
            d2, on_scalar = d2s.pop(panel)
            nc.scalar.activation(
                out=dist[g, h][
                    :, tiles[0] : tiles[-1] + 1, rows[0] * P : (rows[-1] + 1) * P
                ],
                in_=d2[:],
                func=ACT.Sqrt,
                bias=floor[:] if on_scalar else 0.0,
            )

        def transpose_words(row_words):
            bank = psum.tile([P, GROUP, WORDS], F32, tag="bank", name="word_bank")
            for r in range(GROUP_TILES):
                for w in range(WORDS):
                    nc.tensor.transpose(
                        bank[:, r * P : (r + 1) * P, w], row_words(r)[:, w::WORDS], ident_f32[:]
                    )
            return bank

        def transpose_pf(q, g):
            return transpose_words(lambda r: pf_sb[q, g][:, r, :].bitcast(F32))

        def new_force():
            return work.tile([P, GROUP * PACK], BF16, tag="force", align_bytes=64, name="force")

        def multiply(q, g, pfT, force, row_tiles=range(GROUP_TILES)):
            h, w_row = divmod(q, WORDS)
            rows = slice(row_tiles[0] * P, (row_tiles[-1] + 1) * P)
            cols = slice(w_row * GROUP + rows.start, w_row * GROUP + rows.stop)
            nc.vector.tensor_tensor(
                out=force[:, rows.start * PACK : rows.stop * PACK].rearrange(
                    "p (n i t) -> p n t i", i=RUN, t=PACK
                ),
                in0=dist[g, h][:, :, cols].rearrange("p t (n i) -> p n t i", i=RUN),
                in1=pfT[:, rows, :].rearrange("p n w -> p (n w)").bitcast(BF16).rearrange(
                    "p (n i t) -> p n t i", i=RUN, t=PACK
                ),
                op=ALU.mult,
            )
            return force

        force_rows = {}

        def multiply_rows(q, g, r, engine):
            h, w_row = divmod(q, WORDS)
            product = keep.tile([P, HALF], BF16, name="rows_%d_%d_%d" % (q, g, r))
            engine.tensor_tensor(
                out=product[:].rearrange("p (m i u) -> p m u i", i=RUN, u=PACK),
                in0=dist[h, g][:, w_row * PAIR + r, :].rearrange(
                    "p (u m i) -> p m u i", u=PACK, i=RUN
                ),
                in1=pf_sb[q, g][:, r, :].rearrange("p (m i u) -> p m u i", i=RUN, u=PACK),
                op=ALU.mult,
            )
            force_rows[q, g, r] = product

        def transpose_force(q, g):
            return transpose_words(lambda r: force_rows[q, g, r][:].bitcast(F32))

        def group_force(forceT):
            force = work.tile([P, GROUP * PACK], BF16, tag="force", align_bytes=64, name="force")
            nc.scalar.copy(
                out=force[:].bitcast(F32),
                in_=forceT[:].rearrange("p n w -> p (n w)"),
            )
            return force

        codes = {}

        def quantise(q, g, force, row_tiles=range(GROUP_TILES)):
            if (q, g) not in codes:
                codes[q, g] = (
                    keep.tile([P, GROUP], U32, name="codes_%d_%d" % (q, g), align_bytes=64),
                    keep.tile([P, GROUP], U8, name="scales_%d_%d" % (q, g), align_bytes=64),
                )
            packed, scales = codes[q, g]
            rows = slice(row_tiles[0] * P, (row_tiles[-1] + 1) * P)
            nc.vector.quantize_mx(
                out=packed[:, rows].bitcast(FP8X4),
                scales=scales[:, rows],
                in_=force[:, rows.start * PACK : rows.stop * PACK],
            )

        acc = {}

        def multiply_members(q, g, first):
            packed, scales = codes[q, g]
            for r in range(GROUP_TILES):
                if first:
                    acc[q, r] = psum.tile([P, CLUSTERS], F32, tag="bank", name="acc_bank")
                nc.tensor.matmul_mx(
                    out=acc[q, r][:],
                    lhsT=packed[:, r * P : (r + 1) * P].bitcast(FP8X4),
                    lhsT_scale=scales[:, r * P : (r + 1) * P],
                    rhs=members_codes[:, g, :].bitcast(FP8X4),
                    rhs_scale=members_scales[:, g, :],
                    start=first,
                    stop=not first,
                )

        def store(q, r, engine_copy):
            h, w_row = divmod(q, WORDS)
            result = keep.tile([P, CLUSTERS], F32, name="result_%d_%d" % (q, r))
            engine_copy(out=result[:], in_=acc[q, r][:])
            nc.sync.dma_start(out=out_rows[:, h, w_row, r, :], in_=result[:])

        full = range(PACK)
        upper = range(GROUP_TILES, PACK)
        p01 = [(0, 1, (t,), tuple(full)) for t in full]
        p00 = [(0, 0, (t,), tuple(full)) for t in range(GROUP_TILES)] + [(0, 0, tuple(upper), tuple(upper))]
        p11 = [(1, 1, (t,), tuple(full)) for t in range(GROUP_TILES)] + [(1, 1, tuple(upper), tuple(upper))]
        gram(p01[0])
        gram(p01[1])
        nc.scalar.copy(out=featsT[:, 0:P], in_=featsT_0a[:])
        nc.scalar.copy(out=featsT[:, P:HALF], in_=featsT_0b[:])
        nc.scalar.mul(out=featsT_m2[:, half_cols[1]], in_=featsT_1[:], mul=-2.0)
        group_members(0)
        subtract_floor()
        gram(p01[2])
        clamp(p01[0])
        gram(p01[3])
        clamp(p01[1])
        root(p01[0])
        clamp(p01[2])
        root(p01[1])
        gram(p00[0])
        root(p01[2])
        multiply_rows(0, 1, 0, nc.gpsimd)
        clamp(p01[3])
        gram(p00[2])
        root(p01[3])
        group_members(1)
        clamp(p00[0])
        root(p00[0])
        pfT20 = transpose_pf(2, 0)
        clamp(p00[2])
        gram(p00[1])
        pfT30 = transpose_pf(3, 0)
        keep_clock(featsT)
        root(p00[2])
        clamp(p00[1], True)
        root(p00[1])
        f20 = multiply(2, 0, pfT20, new_force())
        pfT10 = transpose_pf(1, 0)
        gram(p11[0])
        f30 = multiply(3, 0, pfT30, new_force())
        gram(p11[1])
        clamp(p11[0], True)
        root(p11[0])
        gram(p11[2])
        clamp(p11[1], True)
        root(p11[1])
        keep_clock(featsT)
        f10 = multiply(1, 0, pfT10, new_force())
        clamp(p11[2], True)
        multiply_rows(0, 1, 1, nc.vector)
        multiply_rows(1, 1, 0, nc.vector)
        multiply_rows(1, 1, 1, nc.vector)
        keep_clock(f10)
        fT01 = transpose_force(0, 1)
        f01 = group_force(fT01)
        keep_clock(force_rows[1, 1, 0])
        fT11 = transpose_force(1, 1)
        root(p11[2])
        f11 = group_force(fT11)
        quantise_members(0)
        quantise(1, 0, f10)
        quantise(2, 0, f20)
        multiply_members(1, 0, True)
        multiply_members(2, 0, True)
        multiply_rows(2, 1, 0, nc.vector)
        multiply_rows(2, 1, 1, nc.vector)
        fT21 = transpose_force(2, 1)
        f21 = group_force(fT21)
        pfT31 = transpose_pf(3, 1)
        quantise_members(1)
        quantise(1, 1, f11)
        multiply_members(1, 1, False)
        multiply_rows(0, 0, 0, nc.vector)
        multiply_rows(0, 0, 1, nc.vector)
        fT00 = transpose_force(0, 0)
        store(1, 0, nc.scalar.copy)
        store(1, 1, nc.scalar.copy)
        f00 = group_force(fT00)
        quantise(2, 1, f21)
        multiply_members(2, 1, False)
        quantise(0, 1, f01)
        quantise(3, 0, f30)
        multiply_members(0, 1, True)
        multiply_members(3, 0, True)
        f31 = new_force()
        multiply(3, 1, pfT31, f31, (0,))
        store(2, 0, nc.scalar.copy)
        store(2, 1, nc.scalar.copy)
        quantise(0, 0, f00)
        multiply_members(0, 0, False)
        multiply(3, 1, pfT31, f31, (1,))
        quantise(3, 1, f31, (0,))
        quantise(3, 1, f31, (1,))
        multiply_members(3, 1, False)
        store(0, 0, nc.scalar.copy)
        store(0, 1, nc.vector.tensor_copy)
        store(3, 0, nc.scalar.copy)
        store(3, 1, nc.vector.tensor_copy)
